import numpy as np
import ml_dtypes


def mxq(x, axis, fmt="e4m3"):
    dtype, down = {"e4m3": (ml_dtypes.float8_e4m3fn, 7), "e5m2": (ml_dtypes.float8_e5m2, 14)}[fmt]
    v = np.moveaxis(np.asarray(x, np.float32).astype(ml_dtypes.bfloat16).astype(np.float64), axis, -1)
    blocks = v.reshape(v.shape[:-1] + (-1, 32))
    amax = np.abs(blocks).max(-1, keepdims=True)
    byte = np.maximum(np.where(amax > 0, np.frexp(amax)[1] - 1 + 127, 0) - down, 1)
    scale = np.exp2(byte - 127.0)
    codes = (blocks / scale).astype(np.float32).astype(dtype).astype(np.float64)
    return np.moveaxis((codes * scale).reshape(v.shape), -1, axis)


WIDE = False


def mx_kscale(k):
    if not WIDE:
        return np.ones(k)
    levels = np.array([10, -10, 5, -5, 0])
    a = np.random.permutation(np.resize(levels, k // 512 * 4)).reshape(k // 512, 4)
    idx = np.arange(k)
    return np.exp2(a[idx // 512, idx % 128 // 32])


BF16 = ml_dtypes.bfloat16


def bf(x):
    return np.asarray(x, np.float32).astype(BF16)


def f64(x):
    return np.asarray(x).astype(np.float64)


E2M1 = np.array([0.0, 0.5, 1.0, 1.5, 2.0, 3.0, 4.0, 6.0, -0.0, -0.5, -1.0, -1.5, -2.0, -3.0, -4.0, -6.0])


def pack_weight(w, fmt):
    k, n = w.shape
    w = f64(bf(w)).reshape(k // 32, 32, n)
    amax = np.abs(w).max(1)
    if fmt == "e4m3":
        byte = np.frexp(amax)[1] - 1 + 127 - 7
    else:
        mant, ex = np.frexp(amax / 6.0)
        byte = np.where(mant > 0.5, ex, ex - 1) + 127
    byte = np.clip(np.where(amax > 0, byte, 1), 1, 254)
    scaled = (w * np.exp2(127.0 - byte)[:, None, :]).reshape(k, n).astype(np.float32)
    by_word = np.ascontiguousarray(scaled.reshape(k // 512, 128, 4, n).transpose(0, 1, 3, 2))
    if fmt == "e4m3":
        words = by_word.astype(ml_dtypes.float8_e4m3fn).view(np.uint8)
    else:
        c = by_word.astype(ml_dtypes.float4_e2m1fn).view(np.uint8) & 0xF
        words = c[..., 0::2] | (c[..., 1::2] << 4)
    return np.ascontiguousarray(words), np.ascontiguousarray(byte.astype(np.uint8).reshape(k // 512, 16, n))


def unpack_weight(words, scales, fmt):
    g, p, n, _ = words.shape
    if fmt == "e4m3":
        vals = np.ascontiguousarray(words).view(ml_dtypes.float8_e4m3fn).astype(np.float64)
    else:
        nib = np.empty((g, p, n, 4), np.uint8)
        nib[..., 0::2] = words & 0xF
        nib[..., 1::2] = words >> 4
        vals = E2M1[nib]
    vals = vals * np.repeat(np.exp2(scales.astype(np.float64) - 127.0), 8, axis=1)[..., None]
    return vals.transpose(0, 1, 3, 2).reshape(g * 512, n)

def pack4(w):
    words, scales = pack_weight(w, "e2m1")
    return words.reshape(words.shape[0], 128, -1), scales


def unpack4(words, scales):
    return unpack_weight(words.reshape(words.shape[0], 128, -1, 2), scales, "e2m1")


B, F, DOF, N_CLS = 256, 256, 64, 1024
K = F * DOF


def setup_inputs():
    s = mx_kscale(K)
    c = s.max() / s.min()
    far = (s.reshape(F, 2, 32)[:, :, 0] == s.max()) & (c > 1.0)
    far[:, 1] &= ~far[:, 0]
    lo, hi = -3.0 / c, 3.0
    pos = 0.5 + np.random.standard_normal((B, F)) / 6.0
    pos = np.where(far[:, 1], 0.48 * np.minimum(pos, 1.0), pos)
    pos = np.where(far[:, 0], 1.0 - 0.48 * (1.0 - np.maximum(pos, 0.0)), pos)
    xv = f64(bf(lo + (hi - lo) * pos))
    xv[xv == hi] = 2.5
    xv[xv == lo] = -2.5
    wf = (np.where(far, c, 1.0)[:, :, None] * np.ones(32)).reshape(K)
    w_nk = np.random.standard_normal((N_CLS, K)) * 0.005 * wf
    words, scales = pack4(np.ascontiguousarray(w_nk.T))
    return {"x": bf(xv), "min_x": bf(np.array([lo])), "max_x": bf(np.array([hi])),
            "W_words": words, "W_scales": scales, "dof": DOF}


def _lagrange_embed(x, min_x, max_x, dof):
    b_, f_ = x.shape
    T = dof - 1
    h = 1.0 / T
    xn = ((x.reshape(-1, 1) - min_x) / (max_x - min_x)).reshape(-1)
    t = np.arange(T, dtype=np.float64)
    s = xn[:, None] / h
    lam0 = s - t
    lam1 = (t + 1.0) - s
    n2t = ((lam0 >= 0.0) & (lam1 >= 0.0)).astype(np.float64)
    z = np.zeros((xn.shape[0], 1), dtype=np.float64)
    mask = np.concatenate([n2t, z], axis=1) + np.concatenate([z, n2t], axis=1)
    w0 = n2t * lam0
    w1 = n2t * lam1
    shape_vals = np.concatenate([w1, z], axis=1) + np.concatenate([z, w0], axis=1)
    basis = shape_vals / np.maximum(mask, 1.0)
    emb = basis * (max_x - min_x) + min_x
    return emb.reshape(b_, f_ * dof)


def reference(x, min_x, max_x, W_words, W_scales, dof):
    emb = _lagrange_embed(f64(x), f64(min_x), f64(max_x), int(dof))
    return mxq(emb, 1, "e4m3") @ unpack4(W_words, W_scales)

@@ -1,0 +1,214 @@
+from contextlib import ExitStack
+
+import concourse.mybir as mybir
+from concourse.masks import make_identity
+
+F32 = mybir.dt.float32
+BF16 = mybir.dt.bfloat16
+I32 = mybir.dt.int32
+U32 = mybir.dt.uint32
+U8 = mybir.dt.uint8
+FP8X4 = mybir.dt.float8_e4m3fn_x4
+FP4X4 = mybir.dt.float4_e2m1fn_x4
+ALU = mybir.AluOpType
+ACT = mybir.ActivationFunctionType
+
+P = 128
+B = 256
+F = 256
+DOF = 64
+N_CLS = 1024
+K = F * DOF
+GROUPS = K // 512
+PAIRS = GROUPS // 2
+SUPER = 8
+FLOPS = 2 * B * K * N_CLS
+
+
+def tile_lagrangenet_kernel(tc, x, min_x, max_x, W_words, W_scales, dof, out):
+    nc = tc.nc
+    assert dof == DOF
+    with ExitStack() as ctx:
+        const = ctx.enter_context(tc.tile_pool(name="const", bufs=1))
+        wpool = ctx.enter_context(tc.tile_pool(name="wpool", bufs=1))
+        cpool = ctx.enter_context(tc.tile_pool(name="cpool", bufs=1))
+        apool = ctx.enter_context(tc.tile_pool(name="apool", bufs=4))
+        epool = ctx.enter_context(tc.tile_pool(name="epool", bufs=3))
+        opool = ctx.enter_context(tc.tile_pool(name="opool", bufs=1))
+        accp = ctx.enter_context(tc.psum_pool(name="accp", bufs=1))
+        repp = ctx.enter_context(tc.psum_pool(name="repp", bufs=4))
+        ctx.enter_context(tc.manual_schedule())
+
+        ident = const.tile([P, P], BF16, name="ident")
+        sel = const.tile([P, P * 16], BF16, name="sel")
+        vidx = const.tile([P, 4], I32, name="vidx")
+        vmod = const.tile([P, 4], I32, name="vmod")
+        vneg = const.tile([P, 4], F32, name="vneg")
+        bias = const.tile([P, 4], F32, name="bias")
+        sc = const.tile([P, 4], F32, name="sc")
+        mn_bf = const.tile([P, 1], BF16, name="mn_bf")
+        mx_bf = const.tile([P, 1], BF16, name="mx_bf")
+        zero = const.tile([P, 1], F32, name="zero")
+        junk = const.tile([P, 1], F32, name="junk")
+        x_sb = [const.tile([P, 2, P], BF16, name="x_sb%d" % c) for c in range(2)]
+        xT = [const.tile([P, B], BF16, name="xT%d" % c) for c in range(2)]
+        below = [const.tile([P, B], F32, name="below%d" % c) for c in range(2)]
+        side = [const.tile([P, B], F32, name="side%d" % c) for c in range(2)]
+        words = [wpool.tile([P, 2, 2 * N_CLS], U8, name="words%d" % j, align_bytes=64) for j in range(PAIRS)]
+        planes = [wpool.tile([P, SUPER, N_CLS], U8, name="planes%d" % s, align_bytes=64) for s in range(3)]
+        codes = [cpool.tile([P, 512], U32, name="codes%d" % j, align_bytes=64) for j in range(PAIRS)]
+        eplane = [cpool.tile([P, 512], U8, name="eplane%d" % j, align_bytes=64) for j in range(PAIRS)]
+        acc = [[accp.tile([P, 512], F32, name="acc%d%d" % (h, nh)) for nh in range(2)] for h in range(2)]
+
+        mx32 = sc[:, 0:1]
+        negmn = sc[:, 1:2]
+        rng = sc[:, 2:3]
+        c0 = sc[:, 3:4]
+
+        nc.vector.memset(zero[:], 0.0)
+        make_identity(nc, ident[:])
+        nc.gpsimd.iota(vidx[:], pattern=[[1, 4]], base=0, channel_multiplier=4)
+        with nc.allow_non_contiguous_dma(reason="one bf16 scalar to every partition"):
+            nc.scalar.dma_start(out=mn_bf[:], in_=min_x.partition_broadcast(P))
+            nc.scalar.dma_start(out=mx_bf[:], in_=max_x.partition_broadcast(P))
+        x_v = x.rearrange("(h p) f -> p h f", p=P)
+        for c in range(2):
+            nc.sync.dma_start(out=x_sb[c][:], in_=x_v[:, :, c * P:(c + 1) * P])
+        for s in range(3):
+            nc.vector.memset(planes[s][:].bitcast(I32), 0)
+
+        def load_super(s):
+            pl = planes[s % 3]
+            g0 = s * SUPER
+            for b in range(2):
+                for r in range(4):
+                    nc.sync.dma_start(
+                        out=pl[32 * b + r:P:64, :, :].bitcast(I32),
+                        in_=W_scales[g0:g0 + SUPER, 4 * b + r:16:8, :].bitcast(I32).rearrange("g q n -> q g n"),
+                    )
+            for j in range(g0 // 2, (g0 + SUPER) // 2):
+                nc.sync.dma_start(
+                    out=words[j][:].bitcast(I32),
+                    in_=W_words[2 * j:2 * j + 2].bitcast(I32).rearrange("g p n -> p g n"),
+                )
+
+        for s in range(3):
+            load_super(s)
+
+        nc.scalar.activation(out=junk[:], in_=zero[:], func=ACT.Abs)
+        nc.scalar.copy(
+            out=sel[:].rearrange("p (f r) -> p f r", r=16),
+            in_=ident[:].unsqueeze(2).to_broadcast([P, P, 16]),
+        )
+
+        nc.vector.tensor_single_scalar(out=vmod[:], in_=vidx[:], scalar=63, op=ALU.bitwise_and)
+        nc.vector.tensor_scalar(out=vneg[:], in0=vmod[:], scalar1=-1.0, scalar2=None, op0=ALU.mult)
+        nc.vector.tensor_tensor(out=rng, in0=mx_bf[:], in1=mn_bf[:], op=ALU.subtract)
+        nc.vector.tensor_scalar(out=c0, in0=mn_bf[:], scalar1=-63.0, scalar2=None, op0=ALU.mult)
+        nc.vector.tensor_scalar(out=bias[:], in0=vneg[:], scalar1=rng, scalar2=c0, op0=ALU.mult, op1=ALU.add)
+        nc.vector.tensor_copy(out=mx32, in_=mx_bf[:])
+        nc.vector.tensor_scalar(out=negmn, in0=mn_bf[:], scalar1=-1.0, scalar2=None, op0=ALU.mult)
+
+        tps = []
+        for c in range(2):
+            tp = repp.tile([P, B], BF16, name="tp%d" % c, tag="rep")
+            for h in range(2):
+                nc.tensor.transpose(tp[:, h * P:(h + 1) * P], x_sb[c][:, h, :], ident[:])
+            tps.append(tp)
+        for c in range(2):
+            nc.vector.tensor_scalar(out=below[c][:], in0=tps[c][:], scalar1=mn_bf[:], scalar2=None, op0=ALU.is_lt)
+            nc.vector.scalar_tensor_tensor(
+                out=side[c][:], in0=tps[c][:], scalar=mx_bf[:], in1=below[c][:], op0=ALU.is_gt, op1=ALU.subtract
+            )
+            nc.vector.scalar_tensor_tensor(
+                out=xT[c][:], in0=side[c][:], scalar=rng, in1=tps[c][:], op0=ALU.mult, op1=ALU.add
+            )
+
+        reps = {}
+        atiles = {}
+        etiles = {}
+
+        def rep(j):
+            rp = repp.tile([P, 512], F32, name="rep%d" % j, tag="rep")
+            for gg in range(2):
+                g = 2 * j + gg
+                blk = g % 16
+                nc.tensor.matmul(
+                    out=rp[:, gg * B:(gg + 1) * B],
+                    lhsT=sel[:, blk * P:(blk + 1) * P],
+                    rhs=xT[g // 16][:],
+                    start=True,
+                    stop=True,
+                )
+            reps[j] = rp
+
+        def dist(j):
+            a = apool.tile([P, 4, 512], F32, name="a%d" % j, tag="a")
+            for t in range(4):
+                nc.scalar.activation(out=a[:, t, :], in_=reps[j][:], func=ACT.Abs, bias=bias[:, t:t + 1], scale=63.0)
+            atiles[j] = a
+
+        def hat(j):
+            e = epool.tile([P, 512, 4], BF16, name="e%d" % j, tag="e", align_bytes=64)
+            nc.vector.tensor_scalar(
+                out=e[:],
+                in0=atiles[j][:].rearrange("p t n -> p n t"),
+                scalar1=mx32,
+                scalar2=negmn,
+                op0=ALU.subtract,
+                op1=ALU.min,
+            )
+            etiles[j] = e
+
+        def quant(j):
+            nc.vector.quantize_mx(
+                out=codes[j][:].bitcast(FP8X4),
+                scales=eplane[j][:],
+                in_=etiles[j][:].rearrange("p n t -> p (n t)"),
+            )
+
+        def one_pass(j, gg, h, nh):
+            g = 2 * j + gg
+            cols = slice(gg * B + h * P, gg * B + (h + 1) * P)
+            nc.tensor.matmul_mx(
+                out=acc[h][nh][:],
+                lhsT=codes[j][:, cols].bitcast(FP8X4),
+                lhsT_scale=eplane[j][:, cols],
+                rhs=words[j][:, gg, nh * N_CLS:(nh + 1) * N_CLS].bitcast(FP4X4),
+                rhs_scale=planes[(g // SUPER) % 3][:, g % SUPER, nh * 512:(nh + 1) * 512],
+                start=(g == 0),
+                stop=(g == GROUPS - 1),
+            )
+
+        def mx(j):
+            if j < PAIRS - 1:
+                for gg in range(2):
+                    for h in range(2):
+                        for nh in range(2):
+                            one_pass(j, gg, h, nh)
+            else:
+                for h in range(2):
+                    for nh in range(2):
+                        for gg in range(2):
+                            one_pass(j, gg, h, nh)
+
+        for j in range(4):
+            rep(j)
+        for j in range(PAIRS):
+            dist(j)
+            hat(j)
+            quant(j)
+            mx(j)
+            if j == 3:
+                load_super(3)
+            if j + 4 < PAIRS:
+                rep(j + 4)
+
+        for h in range(2):
+            for nh in range(2):
+                o = opool.tile([P, 512], F32, name="o%d%d" % (h, nh))
+                if nh == 0:
+                    nc.scalar.mul(out=o[:], in_=acc[h][nh][:], mul=-1.0)
+                else:
+                    nc.vector.tensor_scalar(out=o[:], in0=acc[h][nh][:], scalar1=-1.0, scalar2=None, op0=ALU.mult)
+                nc.sync.dma_start(out=out[h * P:(h + 1) * P, nh * 512:(nh + 1) * 512], in_=o[:])

@@ -32,8 +32,8 @@ def tile_lagrangenet_kernel(tc, x, min_x, max_x, W_words, W_scales, dof, out):
         const = ctx.enter_context(tc.tile_pool(name="const", bufs=1))
         wpool = ctx.enter_context(tc.tile_pool(name="wpool", bufs=1))
         cpool = ctx.enter_context(tc.tile_pool(name="cpool", bufs=1))
-        apool = ctx.enter_context(tc.tile_pool(name="apool", bufs=4))
-        epool = ctx.enter_context(tc.tile_pool(name="epool", bufs=3))
+        apool = ctx.enter_context(tc.tile_pool(name="apool", bufs=6))
+        epool = ctx.enter_context(tc.tile_pool(name="epool", bufs=4))
         opool = ctx.enter_context(tc.tile_pool(name="opool", bufs=1))
         accp = ctx.enter_context(tc.psum_pool(name="accp", bufs=1))
         repp = ctx.enter_context(tc.psum_pool(name="repp", bufs=4))
@@ -50,14 +50,14 @@ def tile_lagrangenet_kernel(tc, x, min_x, max_x, W_words, W_scales, dof, out):
         mx_bf = const.tile([P, 1], BF16, name="mx_bf")
         zero = const.tile([P, 1], F32, name="zero")
         junk = const.tile([P, 1], F32, name="junk")
-        x_sb = [const.tile([P, 2, P], BF16, name="x_sb%d" % c) for c in range(2)]
+        x_sb = const.tile([P, 2, F], BF16, name="x_sb")
         xT = [const.tile([P, B], BF16, name="xT%d" % c) for c in range(2)]
         below = [const.tile([P, B], F32, name="below%d" % c) for c in range(2)]
         side = [const.tile([P, B], F32, name="side%d" % c) for c in range(2)]
         words = [wpool.tile([P, 2, 2 * N_CLS], U8, name="words%d" % j, align_bytes=64) for j in range(PAIRS)]
         planes = [wpool.tile([P, SUPER, N_CLS], U8, name="planes%d" % s, align_bytes=64) for s in range(3)]
-        codes = [cpool.tile([P, 512], U32, name="codes%d" % j, align_bytes=64) for j in range(PAIRS)]
-        eplane = [cpool.tile([P, 512], U8, name="eplane%d" % j, align_bytes=64) for j in range(PAIRS)]
+        codes = [cpool.tile([P, B], U32, name="codes%d" % g, align_bytes=64) for g in range(GROUPS)]
+        eplane = [cpool.tile([P, B], U8, name="eplane%d" % g, align_bytes=64) for g in range(GROUPS)]
         acc = [[accp.tile([P, 512], F32, name="acc%d%d" % (h, nh)) for nh in range(2)] for h in range(2)]
 
         mx32 = sc[:, 0:1]
@@ -71,35 +71,44 @@ def tile_lagrangenet_kernel(tc, x, min_x, max_x, W_words, W_scales, dof, out):
         with nc.allow_non_contiguous_dma(reason="one bf16 scalar to every partition"):
             nc.scalar.dma_start(out=mn_bf[:], in_=min_x.partition_broadcast(P))
             nc.scalar.dma_start(out=mx_bf[:], in_=max_x.partition_broadcast(P))
-        x_v = x.rearrange("(h p) f -> p h f", p=P)
-        for c in range(2):
-            nc.sync.dma_start(out=x_sb[c][:], in_=x_v[:, :, c * P:(c + 1) * P])
-        for s in range(3):
-            nc.vector.memset(planes[s][:].bitcast(I32), 0)
+        nc.sync.dma_start(out=x_sb[:], in_=x.rearrange("(h p) f -> p h f", p=P))
+        nc.vector.memset(planes[0][:, 0:4, :].bitcast(I32), 0)
+        nc.vector.memset(planes[0][:, 4:8, :].bitcast(I32), 0)
+        nc.gpsimd.memset(planes[1][:].bitcast(F32), 0.0)
+        nc.gpsimd.memset(planes[2][:].bitcast(F32), 0.0)
 
-        def load_super(s):
-            pl = planes[s % 3]
-            g0 = s * SUPER
-            for b in range(2):
-                for r in range(4):
-                    nc.sync.dma_start(
-                        out=pl[32 * b + r:P:64, :, :].bitcast(I32),
-                        in_=W_scales[g0:g0 + SUPER, 4 * b + r:16:8, :].bitcast(I32).rearrange("g q n -> q g n"),
-                    )
-            for j in range(g0 // 2, (g0 + SUPER) // 2):
+        def load_scales(g0, g1, cut):
+            pl = planes[(g0 // SUPER) % 3]
+            for r0 in range(16 // cut):
+                part = 32 * (r0 // 4) + r0 % 4
                 nc.sync.dma_start(
-                    out=words[j][:].bitcast(I32),
-                    in_=W_words[2 * j:2 * j + 2].bitcast(I32).rearrange("g p n -> p g n"),
+                    out=pl[part:P:P // cut, g0 % SUPER:(g1 - 1) % SUPER + 1, :].bitcast(I32),
+                    in_=W_scales[g0:g1, r0:16:16 // cut, :].bitcast(I32).rearrange("g q n -> q g n"),
                 )
 
-        for s in range(3):
-            load_super(s)
+        def load_words(j):
+            nc.sync.dma_start(
+                out=words[j][:].bitcast(I32),
+                in_=W_words[2 * j:2 * j + 2].bitcast(I32).rearrange("g p n -> p g n"),
+            )
+
+        load_scales(0, 4, 4)
+        load_words(0)
+        load_words(1)
+        load_scales(4, 8, 4)
+        load_words(2)
+        load_words(3)
+        for s in range(1, 3):
+            load_scales(s * SUPER, (s + 1) * SUPER, 2)
+            for j in range(4 * s, 4 * s + 4):
+                load_words(j)
 
         nc.scalar.activation(out=junk[:], in_=zero[:], func=ACT.Abs)
-        nc.scalar.copy(
-            out=sel[:].rearrange("p (f r) -> p f r", r=16),
-            in_=ident[:].unsqueeze(2).to_broadcast([P, P, 16]),
-        )
+        for half in range(2):
+            nc.scalar.copy(
+                out=sel[:, half * 1024:(half + 1) * 1024].rearrange("p (f r) -> p f r", r=16),
+                in_=ident[:, half * 64:(half + 1) * 64].unsqueeze(2).to_broadcast([P, 64, 16]),
+            )
 
         nc.vector.tensor_single_scalar(out=vmod[:], in_=vidx[:], scalar=63, op=ALU.bitwise_and)
         nc.vector.tensor_scalar(out=vneg[:], in0=vmod[:], scalar1=-1.0, scalar2=None, op0=ALU.mult)
@@ -113,7 +122,7 @@ def tile_lagrangenet_kernel(tc, x, min_x, max_x, W_words, W_scales, dof, out):
         for c in range(2):
             tp = repp.tile([P, B], BF16, name="tp%d" % c, tag="rep")
             for h in range(2):
-                nc.tensor.transpose(tp[:, h * P:(h + 1) * P], x_sb[c][:, h, :], ident[:])
+                nc.tensor.transpose(tp[:, h * P:(h + 1) * P], x_sb[:, h, c * P:(c + 1) * P], ident[:])
             tps.append(tp)
         for c in range(2):
             nc.vector.tensor_scalar(out=below[c][:], in0=tps[c][:], scalar1=mn_bf[:], scalar2=None, op0=ALU.is_lt)
@@ -128,81 +137,66 @@ def tile_lagrangenet_kernel(tc, x, min_x, max_x, W_words, W_scales, dof, out):
         atiles = {}
         etiles = {}
 
-        def rep(j):
-            rp = repp.tile([P, 512], F32, name="rep%d" % j, tag="rep")
-            for gg in range(2):
-                g = 2 * j + gg
-                blk = g % 16
-                nc.tensor.matmul(
-                    out=rp[:, gg * B:(gg + 1) * B],
-                    lhsT=sel[:, blk * P:(blk + 1) * P],
-                    rhs=xT[g // 16][:],
-                    start=True,
-                    stop=True,
-                )
-            reps[j] = rp
+        def rep(g):
+            rp = repp.tile([P, B], F32, name="rep%d" % g, tag="rep")
+            blk = g % 16
+            nc.tensor.matmul(
+                out=rp[:], lhsT=sel[:, blk * P:(blk + 1) * P], rhs=xT[g // 16][:], start=True, stop=True
+            )
+            reps[g] = rp
 
-        def dist(j):
-            a = apool.tile([P, 4, 512], F32, name="a%d" % j, tag="a")
+        def dist(g):
+            a = apool.tile([P, 4, B], F32, name="a%d" % g, tag="a")
             for t in range(4):
-                nc.scalar.activation(out=a[:, t, :], in_=reps[j][:], func=ACT.Abs, bias=bias[:, t:t + 1], scale=63.0)
-            atiles[j] = a
+                nc.scalar.activation(out=a[:, t, :], in_=reps[g][:], func=ACT.Abs, bias=bias[:, t:t + 1], scale=63.0)
+            atiles[g] = a
 
-        def hat(j):
-            e = epool.tile([P, 512, 4], BF16, name="e%d" % j, tag="e", align_bytes=64)
+        def hat(g):
+            e = epool.tile([P, B, 4], BF16, name="e%d" % g, tag="e", align_bytes=64)
             nc.vector.tensor_scalar(
                 out=e[:],
-                in0=atiles[j][:].rearrange("p t n -> p n t"),
+                in0=atiles[g][:].rearrange("p t n -> p n t"),
                 scalar1=mx32,
                 scalar2=negmn,
                 op0=ALU.subtract,
                 op1=ALU.min,
             )
-            etiles[j] = e
+            etiles[g] = e
 
-        def quant(j):
+        def quant(g):
             nc.vector.quantize_mx(
-                out=codes[j][:].bitcast(FP8X4),
-                scales=eplane[j][:],
-                in_=etiles[j][:].rearrange("p n t -> p (n t)"),
+                out=codes[g][:].bitcast(FP8X4),
+                scales=eplane[g][:],
+                in_=etiles[g][:].rearrange("p n t -> p (n t)"),
             )
 
-        def one_pass(j, gg, h, nh):
-            g = 2 * j + gg
-            cols = slice(gg * B + h * P, gg * B + (h + 1) * P)
-            nc.tensor.matmul_mx(
-                out=acc[h][nh][:],
-                lhsT=codes[j][:, cols].bitcast(FP8X4),
-                lhsT_scale=eplane[j][:, cols],
-                rhs=words[j][:, gg, nh * N_CLS:(nh + 1) * N_CLS].bitcast(FP4X4),
-                rhs_scale=planes[(g // SUPER) % 3][:, g % SUPER, nh * 512:(nh + 1) * 512],
-                start=(g == 0),
-                stop=(g == GROUPS - 1),
-            )
+        def mx(g):
+            for h in range(2):
+                for nh in range(2):
+                    cols = slice(h * P, (h + 1) * P)
+                    nc.tensor.matmul_mx(
+                        out=acc[h][nh][:],
+                        lhsT=codes[g][:, cols].bitcast(FP8X4),
+                        lhsT_scale=eplane[g][:, cols],
+                        rhs=words[g // 2][:, g % 2, nh * N_CLS:(nh + 1) * N_CLS].bitcast(FP4X4),
+                        rhs_scale=planes[(g // SUPER) % 3][:, g % SUPER, nh * 512:(nh + 1) * 512],
+                        start=(g == 0),
+                        stop=(g == GROUPS - 1),
+                    )
 
-        def mx(j):
-            if j < PAIRS - 1:
-                for gg in range(2):
-                    for h in range(2):
-                        for nh in range(2):
-                            one_pass(j, gg, h, nh)
-            else:
-                for h in range(2):
-                    for nh in range(2):
-                        for gg in range(2):
-                            one_pass(j, gg, h, nh)
-
-        for j in range(4):
-            rep(j)
-        for j in range(PAIRS):
-            dist(j)
-            hat(j)
-            quant(j)
-            mx(j)
-            if j == 3:
-                load_super(3)
-            if j + 4 < PAIRS:
-                rep(j + 4)
+        for g in range(4):
+            rep(g)
+        for g in range(GROUPS):
+            dist(g)
+            hat(g)
+            quant(g)
+            mx(g)
+            if g == SUPER - 1:
+                load_scales(3 * SUPER, 4 * SUPER, 2)
+                for j in range(12, 16):
+                    load_words(j)
+            if g + 4 < GROUPS:
+                rep(g + 4)
 
         for h in range(2):
             for nh in range(2):

@@ -32,7 +32,7 @@ def tile_lagrangenet_kernel(tc, x, min_x, max_x, W_words, W_scales, dof, out):
         const = ctx.enter_context(tc.tile_pool(name="const", bufs=1))
         wpool = ctx.enter_context(tc.tile_pool(name="wpool", bufs=1))
         cpool = ctx.enter_context(tc.tile_pool(name="cpool", bufs=1))
-        apool = ctx.enter_context(tc.tile_pool(name="apool", bufs=6))
+        apool = ctx.enter_context(tc.tile_pool(name="apool", bufs=4))
         epool = ctx.enter_context(tc.tile_pool(name="epool", bufs=4))
         opool = ctx.enter_context(tc.tile_pool(name="opool", bufs=1))
         accp = ctx.enter_context(tc.psum_pool(name="accp", bufs=1))
@@ -55,7 +55,7 @@ def tile_lagrangenet_kernel(tc, x, min_x, max_x, W_words, W_scales, dof, out):
         below = [const.tile([P, B], F32, name="below%d" % c) for c in range(2)]
         side = [const.tile([P, B], F32, name="side%d" % c) for c in range(2)]
         words = [wpool.tile([P, 2, 2 * N_CLS], U8, name="words%d" % j, align_bytes=64) for j in range(PAIRS)]
-        planes = [wpool.tile([P, SUPER, N_CLS], U8, name="planes%d" % s, align_bytes=64) for s in range(3)]
+        planes = [wpool.tile([P, SUPER, N_CLS], U8, name="planes%d" % s, align_bytes=64) for s in range(2)]
         codes = [cpool.tile([P, B], U32, name="codes%d" % g, align_bytes=64) for g in range(GROUPS)]
         eplane = [cpool.tile([P, B], U8, name="eplane%d" % g, align_bytes=64) for g in range(GROUPS)]
         acc = [[accp.tile([P, 512], F32, name="acc%d%d" % (h, nh)) for nh in range(2)] for h in range(2)]
@@ -72,13 +72,10 @@ def tile_lagrangenet_kernel(tc, x, min_x, max_x, W_words, W_scales, dof, out):
             nc.scalar.dma_start(out=mn_bf[:], in_=min_x.partition_broadcast(P))
             nc.scalar.dma_start(out=mx_bf[:], in_=max_x.partition_broadcast(P))
         nc.sync.dma_start(out=x_sb[:], in_=x.rearrange("(h p) f -> p h f", p=P))
-        nc.vector.memset(planes[0][:, 0:4, :].bitcast(I32), 0)
-        nc.vector.memset(planes[0][:, 4:8, :].bitcast(I32), 0)
-        nc.gpsimd.memset(planes[1][:].bitcast(F32), 0.0)
-        nc.gpsimd.memset(planes[2][:].bitcast(F32), 0.0)
+        nc.vector.memset(planes[0][:].bitcast(I32), 0)
 
         def load_scales(g0, g1, cut):
-            pl = planes[(g0 // SUPER) % 3]
+            pl = planes[(g0 // SUPER) % 2]
             for r0 in range(16 // cut):
                 part = 32 * (r0 // 4) + r0 % 4
                 nc.sync.dma_start(
@@ -92,16 +89,9 @@ def tile_lagrangenet_kernel(tc, x, min_x, max_x, W_words, W_scales, dof, out):
                 in_=W_words[2 * j:2 * j + 2].bitcast(I32).rearrange("g p n -> p g n"),
             )
 
-        load_scales(0, 4, 4)
-        load_words(0)
-        load_words(1)
-        load_scales(4, 8, 4)
-        load_words(2)
-        load_words(3)
-        for s in range(1, 3):
-            load_scales(s * SUPER, (s + 1) * SUPER, 2)
-            for j in range(4 * s, 4 * s + 4):
-                load_words(j)
+        load_scales(0, SUPER, 2)
+        for j in range(0, 4):
+            load_words(j)
 
         nc.scalar.activation(out=junk[:], in_=zero[:], func=ACT.Abs)
         for half in range(2):
@@ -125,6 +115,11 @@ def tile_lagrangenet_kernel(tc, x, min_x, max_x, W_words, W_scales, dof, out):
                 nc.tensor.transpose(tp[:, h * P:(h + 1) * P], x_sb[:, h, c * P:(c + 1) * P], ident[:])
             tps.append(tp)
         for c in range(2):
+            if c == 1:
+                nc.vector.memset(planes[1][:].bitcast(I32), 0)
+                load_scales(SUPER, 2 * SUPER, 2)
+                for j in range(4, 12):
+                    load_words(j)
             nc.vector.tensor_scalar(out=below[c][:], in0=tps[c][:], scalar1=mn_bf[:], scalar2=None, op0=ALU.is_lt)
             nc.vector.scalar_tensor_tensor(
                 out=side[c][:], in0=tps[c][:], scalar=mx_bf[:], in1=below[c][:], op0=ALU.is_gt, op1=ALU.subtract
@@ -137,25 +132,29 @@ def tile_lagrangenet_kernel(tc, x, min_x, max_x, W_words, W_scales, dof, out):
         atiles = {}
         etiles = {}
 
-        def rep(g):
-            rp = repp.tile([P, B], F32, name="rep%d" % g, tag="rep")
-            blk = g % 16
-            nc.tensor.matmul(
-                out=rp[:], lhsT=sel[:, blk * P:(blk + 1) * P], rhs=xT[g // 16][:], start=True, stop=True
-            )
-            reps[g] = rp
+        def rep(j):
+            rp = repp.tile([P, 2, B], F32, name="rep%d" % j, tag="rep")
+            for gg in range(2):
+                g = 2 * j + gg
+                blk = g % 16
+                nc.tensor.matmul(
+                    out=rp[:, gg, :], lhsT=sel[:, blk * P:(blk + 1) * P], rhs=xT[g // 16][:], start=True, stop=True
+                )
+            reps[j] = rp
 
-        def dist(g):
-            a = apool.tile([P, 4, B], F32, name="a%d" % g, tag="a")
+        def dist(j):
+            a = apool.tile([P, 4, 2, B], F32, name="a%d" % j, tag="a")
             for t in range(4):
-                nc.scalar.activation(out=a[:, t, :], in_=reps[g][:], func=ACT.Abs, bias=bias[:, t:t + 1], scale=63.0)
-            atiles[g] = a
+                nc.scalar.activation(
+                    out=a[:, t, :, :], in_=reps[j][:], func=ACT.Abs, bias=bias[:, t:t + 1], scale=63.0
+                )
+            atiles[j] = a
 
         def hat(g):
             e = epool.tile([P, B, 4], BF16, name="e%d" % g, tag="e", align_bytes=64)
             nc.vector.tensor_scalar(
                 out=e[:],
-                in0=atiles[g][:].rearrange("p t n -> p n t"),
+                in0=atiles[g // 2][:, :, g % 2, :].rearrange("p t n -> p n t"),
                 scalar1=mx32,
                 scalar2=negmn,
                 op0=ALU.subtract,
@@ -179,24 +178,37 @@ def tile_lagrangenet_kernel(tc, x, min_x, max_x, W_words, W_scales, dof, out):
                         lhsT=codes[g][:, cols].bitcast(FP8X4),
                         lhsT_scale=eplane[g][:, cols],
                         rhs=words[g // 2][:, g % 2, nh * N_CLS:(nh + 1) * N_CLS].bitcast(FP4X4),
-                        rhs_scale=planes[(g // SUPER) % 3][:, g % SUPER, nh * 512:(nh + 1) * 512],
+                        rhs_scale=planes[(g // SUPER) % 2][:, g % SUPER, nh * 512:(nh + 1) * 512],
                         start=(g == 0),
                         stop=(g == GROUPS - 1),
                     )
 
-        for g in range(4):
-            rep(g)
-        for g in range(GROUPS):
-            dist(g)
-            hat(g)
-            quant(g)
-            mx(g)
-            if g == SUPER - 1:
+        for j in range(4):
+            rep(j)
+        for j in range(PAIRS):
+            g0 = 2 * j
+            g1 = g0 + 1
+            dist(j)
+            if j == 0:
+                hat(g0)
+                quant(g0)
+                hat(g1)
+                quant(g1)
+            else:
+                hat(g0)
+                hat(g1)
+                quant(g0)
+                quant(g1)
+            mx(g0)
+            mx(g1)
+            if g1 == SUPER - 1:
+                load_scales(2 * SUPER, 3 * SUPER, 2)
+                for jj in range(12, 16):
+                    load_words(jj)
+            if g1 == 2 * SUPER - 1:
                 load_scales(3 * SUPER, 4 * SUPER, 2)
-                for j in range(12, 16):
-                    load_words(j)
-            if g + 4 < GROUPS:
-                rep(g + 4)
+            if j + 4 < PAIRS:
+                rep(j + 4)
 
         for h in range(2):
             for nh in range(2):

@@ -103,10 +103,6 @@ def tile_lagrangenet_kernel(tc, x, min_x, max_x, W_words, W_scales, dof, out):
         nc.vector.tensor_single_scalar(out=vmod[:], in_=vidx[:], scalar=63, op=ALU.bitwise_and)
         nc.vector.tensor_scalar(out=vneg[:], in0=vmod[:], scalar1=-1.0, scalar2=None, op0=ALU.mult)
         nc.vector.tensor_tensor(out=rng, in0=mx_bf[:], in1=mn_bf[:], op=ALU.subtract)
-        nc.vector.tensor_scalar(out=c0, in0=mn_bf[:], scalar1=-63.0, scalar2=None, op0=ALU.mult)
-        nc.vector.tensor_scalar(out=bias[:], in0=vneg[:], scalar1=rng, scalar2=c0, op0=ALU.mult, op1=ALU.add)
-        nc.vector.tensor_copy(out=mx32, in_=mx_bf[:])
-        nc.vector.tensor_scalar(out=negmn, in0=mn_bf[:], scalar1=-1.0, scalar2=None, op0=ALU.mult)
 
         tps = []
         for c in range(2):
@@ -116,10 +112,12 @@ def tile_lagrangenet_kernel(tc, x, min_x, max_x, W_words, W_scales, dof, out):
             tps.append(tp)
         for c in range(2):
             if c == 1:
-                nc.vector.memset(planes[1][:].bitcast(I32), 0)
-                load_scales(SUPER, 2 * SUPER, 2)
-                for j in range(4, 12):
-                    load_words(j)
+                nc.vector.tensor_scalar(out=c0, in0=mn_bf[:], scalar1=-63.0, scalar2=None, op0=ALU.mult)
+                nc.vector.tensor_scalar(
+                    out=bias[:], in0=vneg[:], scalar1=rng, scalar2=c0, op0=ALU.mult, op1=ALU.add
+                )
+                nc.vector.tensor_copy(out=mx32, in_=mx_bf[:])
+                nc.vector.tensor_scalar(out=negmn, in0=mn_bf[:], scalar1=-1.0, scalar2=None, op0=ALU.mult)
             nc.vector.tensor_scalar(out=below[c][:], in0=tps[c][:], scalar1=mn_bf[:], scalar2=None, op0=ALU.is_lt)
             nc.vector.scalar_tensor_tensor(
                 out=side[c][:], in0=tps[c][:], scalar=mx_bf[:], in1=below[c][:], op0=ALU.is_gt, op1=ALU.subtract
@@ -128,25 +126,32 @@ def tile_lagrangenet_kernel(tc, x, min_x, max_x, W_words, W_scales, dof, out):
                 out=xT[c][:], in0=side[c][:], scalar=rng, in1=tps[c][:], op0=ALU.mult, op1=ALU.add
             )
 
+        nc.vector.memset(planes[1][:].bitcast(I32), 0)
+        load_scales(SUPER, 2 * SUPER, 2)
+        for j in range(4, 12):
+            load_words(j)
+
         reps = {}
         atiles = {}
         etiles = {}
 
-        def rep(j):
-            rp = repp.tile([P, 2, B], F32, name="rep%d" % j, tag="rep")
-            for gg in range(2):
-                g = 2 * j + gg
+        rep_sets = [[0, 1]] + [list(range(g, g + 4)) for g in range(2, 30, 4)] + [[30, 31]]
+
+        def rep(m):
+            rp = repp.tile([P, 4, B], BF16, name="rep%d" % m, tag="rep")
+            for i, g in reversed(list(enumerate(rep_sets[m]))):
                 blk = g % 16
                 nc.tensor.matmul(
-                    out=rp[:, gg, :], lhsT=sel[:, blk * P:(blk + 1) * P], rhs=xT[g // 16][:], start=True, stop=True
+                    out=rp[:, i, :], lhsT=sel[:, blk * P:(blk + 1) * P], rhs=xT[g // 16][:], start=True, stop=True
                 )
-            reps[j] = rp
+                if i % 2 == 0:
+                    reps[g // 2] = rp[:, i:i + 2, :]
 
         def dist(j):
             a = apool.tile([P, 4, 2, B], F32, name="a%d" % j, tag="a")
             for t in range(4):
                 nc.scalar.activation(
-                    out=a[:, t, :, :], in_=reps[j][:], func=ACT.Abs, bias=bias[:, t:t + 1], scale=63.0
+                    out=a[:, t, :, :], in_=reps[j], func=ACT.Abs, bias=bias[:, t:t + 1], scale=63.0
                 )
             atiles[j] = a
 
@@ -183,13 +188,15 @@ def tile_lagrangenet_kernel(tc, x, min_x, max_x, W_words, W_scales, dof, out):
                         stop=(g == GROUPS - 1),
                     )
 
-        for j in range(4):
-            rep(j)
+        for m in range(4):
+            rep(m)
+        rep_after = dict((rep_sets[m - 4][-1] // 2, m) for m in range(5, len(rep_sets)))
         for j in range(PAIRS):
             g0 = 2 * j
             g1 = g0 + 1
             dist(j)
             if j == 0:
+                rep(4)
                 hat(g0)
                 quant(g0)
                 hat(g1)
@@ -207,8 +214,8 @@ def tile_lagrangenet_kernel(tc, x, min_x, max_x, W_words, W_scales, dof, out):
                     load_words(jj)
             if g1 == 2 * SUPER - 1:
                 load_scales(3 * SUPER, 4 * SUPER, 2)
-            if j + 4 < PAIRS:
-                rep(j + 4)
+            if j in rep_after:
+                rep(rep_after[j])
 
         for h in range(2):
             for nh in range(2):

@@ -158,8 +158,8 @@ def tile_lagrangenet_kernel(tc, x, min_x, max_x, W_words, W_scales, dof, out):
         def hat(g):
             e = epool.tile([P, B, 4], BF16, name="e%d" % g, tag="e", align_bytes=64)
             nc.vector.tensor_scalar(
-                out=e[:],
-                in0=atiles[g // 2][:, :, g % 2, :].rearrange("p t n -> p n t"),
+                out=e[:].rearrange("p (c i) t -> p c t i", i=4),
+                in0=atiles[g // 2][:, :, g % 2, :].rearrange("p t (c i) -> p c t i", i=4),
                 scalar1=mx32,
                 scalar2=negmn,
                 op0=ALU.subtract,

from contextlib import ExitStack

import concourse.mybir as mybir
from concourse.masks import make_identity

F32 = mybir.dt.float32
BF16 = mybir.dt.bfloat16
I32 = mybir.dt.int32
U32 = mybir.dt.uint32
U8 = mybir.dt.uint8
FP8X4 = mybir.dt.float8_e4m3fn_x4
FP4X4 = mybir.dt.float4_e2m1fn_x4
ALU = mybir.AluOpType
ACT = mybir.ActivationFunctionType

P = 128
B = 256
F = 256
DOF = 64
N_CLS = 1024
K = F * DOF
GROUPS = K // 512
PAIRS = GROUPS // 2
SUPER = 8
FLOPS = 2 * B * K * N_CLS


def tile_lagrangenet_kernel(tc, x, min_x, max_x, W_words, W_scales, dof, out):
    nc = tc.nc
    assert dof == DOF
    with ExitStack() as ctx:
        const = ctx.enter_context(tc.tile_pool(name="const", bufs=1))
        wpool = ctx.enter_context(tc.tile_pool(name="wpool", bufs=1))
        cpool = ctx.enter_context(tc.tile_pool(name="cpool", bufs=1))
        apool = ctx.enter_context(tc.tile_pool(name="apool", bufs=4))
        epool = ctx.enter_context(tc.tile_pool(name="epool", bufs=4))
        opool = ctx.enter_context(tc.tile_pool(name="opool", bufs=1))
        accp = ctx.enter_context(tc.psum_pool(name="accp", bufs=1))
        repp = ctx.enter_context(tc.psum_pool(name="repp", bufs=4))
        ctx.enter_context(tc.manual_schedule())

        ident = const.tile([P, P], BF16, name="ident")
        sel = const.tile([P, P * 16], BF16, name="sel")
        vidx = const.tile([P, 4], I32, name="vidx")
        vmod = const.tile([P, 4], I32, name="vmod")
        vneg = const.tile([P, 4], F32, name="vneg")
        bias = const.tile([P, 4], F32, name="bias")
        sc = const.tile([P, 4], F32, name="sc")
        mn_bf = const.tile([P, 1], BF16, name="mn_bf")
        mx_bf = const.tile([P, 1], BF16, name="mx_bf")
        zero = const.tile([P, 1], F32, name="zero")
        junk = const.tile([P, 1], F32, name="junk")
        x_sb = const.tile([P, 2, F], BF16, name="x_sb")
        xT = [const.tile([P, B], BF16, name="xT%d" % c) for c in range(2)]
        below = [const.tile([P, B], F32, name="below%d" % c) for c in range(2)]
        side = [const.tile([P, B], F32, name="side%d" % c) for c in range(2)]
        words = [wpool.tile([P, 2, 2 * N_CLS], U8, name="words%d" % j, align_bytes=64) for j in range(PAIRS)]
        planes = [wpool.tile([P, SUPER, N_CLS], U8, name="planes%d" % s, align_bytes=64) for s in range(2)]
        codes = [cpool.tile([P, B], U32, name="codes%d" % g, align_bytes=64) for g in range(GROUPS)]
        eplane = [cpool.tile([P, B], U8, name="eplane%d" % g, align_bytes=64) for g in range(GROUPS)]
        acc = [[accp.tile([P, 512], F32, name="acc%d%d" % (h, nh)) for nh in range(2)] for h in range(2)]

        mx32 = sc[:, 0:1]
        negmn = sc[:, 1:2]
        rng = sc[:, 2:3]
        c0 = sc[:, 3:4]

        nc.vector.memset(zero[:], 0.0)
        make_identity(nc, ident[:])
        nc.gpsimd.iota(vidx[:], pattern=[[1, 4]], base=0, channel_multiplier=4)
        with nc.allow_non_contiguous_dma(reason="one bf16 scalar to every partition"):
            nc.scalar.dma_start(out=mn_bf[:], in_=min_x.partition_broadcast(P))
            nc.scalar.dma_start(out=mx_bf[:], in_=max_x.partition_broadcast(P))
        nc.sync.dma_start(out=x_sb[:], in_=x.rearrange("(h p) f -> p h f", p=P))
        nc.vector.memset(planes[0][:].bitcast(I32), 0)

        def load_scales(g0, g1, cut):
            pl = planes[(g0 // SUPER) % 2]
            for r0 in range(16 // cut):
                part = 32 * (r0 // 4) + r0 % 4
                nc.sync.dma_start(
                    out=pl[part:P:P // cut, g0 % SUPER:(g1 - 1) % SUPER + 1, :].bitcast(I32),
                    in_=W_scales[g0:g1, r0:16:16 // cut, :].bitcast(I32).rearrange("g q n -> q g n"),
                )

        def load_words(j):
            nc.sync.dma_start(
                out=words[j][:].bitcast(I32),
                in_=W_words[2 * j:2 * j + 2].bitcast(I32).rearrange("g p n -> p g n"),
            )

        load_scales(0, SUPER, 2)
        for j in range(0, 4):
            load_words(j)

        nc.scalar.activation(out=junk[:], in_=zero[:], func=ACT.Abs)
        for half in range(2):
            nc.scalar.copy(
                out=sel[:, half * 1024:(half + 1) * 1024].rearrange("p (f r) -> p f r", r=16),
                in_=ident[:, half * 64:(half + 1) * 64].unsqueeze(2).to_broadcast([P, 64, 16]),
            )

        nc.vector.tensor_single_scalar(out=vmod[:], in_=vidx[:], scalar=63, op=ALU.bitwise_and)
        nc.vector.tensor_scalar(out=vneg[:], in0=vmod[:], scalar1=-1.0, scalar2=None, op0=ALU.mult)
        nc.vector.tensor_tensor(out=rng, in0=mx_bf[:], in1=mn_bf[:], op=ALU.subtract)

        tps = []
        for c in range(2):
            tp = repp.tile([P, B], BF16, name="tp%d" % c, tag="rep")
            for h in range(2):
                nc.tensor.transpose(tp[:, h * P:(h + 1) * P], x_sb[:, h, c * P:(c + 1) * P], ident[:])
            tps.append(tp)
        for c in range(2):
            if c == 1:
                nc.vector.tensor_scalar(out=c0, in0=mn_bf[:], scalar1=-63.0, scalar2=None, op0=ALU.mult)
                nc.vector.tensor_scalar(
                    out=bias[:], in0=vneg[:], scalar1=rng, scalar2=c0, op0=ALU.mult, op1=ALU.add
                )
                nc.vector.tensor_copy(out=mx32, in_=mx_bf[:])
                nc.vector.tensor_scalar(out=negmn, in0=mn_bf[:], scalar1=-1.0, scalar2=None, op0=ALU.mult)
            nc.vector.tensor_scalar(out=below[c][:], in0=tps[c][:], scalar1=mn_bf[:], scalar2=None, op0=ALU.is_lt)
            nc.vector.scalar_tensor_tensor(
                out=side[c][:], in0=tps[c][:], scalar=mx_bf[:], in1=below[c][:], op0=ALU.is_gt, op1=ALU.subtract
            )
            nc.vector.scalar_tensor_tensor(
                out=xT[c][:], in0=side[c][:], scalar=rng, in1=tps[c][:], op0=ALU.mult, op1=ALU.add
            )

        nc.vector.memset(planes[1][:].bitcast(I32), 0)
        load_scales(SUPER, 2 * SUPER, 2)
        for j in range(4, 12):
            load_words(j)

        reps = {}
        atiles = {}
        etiles = {}

        rep_sets = [[0, 1]] + [list(range(g, g + 4)) for g in range(2, 30, 4)] + [[30, 31]]

        def rep(m):
            rp = repp.tile([P, 4, B], BF16, name="rep%d" % m, tag="rep")
            for i, g in reversed(list(enumerate(rep_sets[m]))):
                blk = g % 16
                nc.tensor.matmul(
                    out=rp[:, i, :], lhsT=sel[:, blk * P:(blk + 1) * P], rhs=xT[g // 16][:], start=True, stop=True
                )
                if i % 2 == 0:
                    reps[g // 2] = rp[:, i:i + 2, :]

        def dist(j):
            a = apool.tile([P, 4, 2, B], F32, name="a%d" % j, tag="a")
            for t in range(4):
                nc.scalar.activation(
                    out=a[:, t, :, :], in_=reps[j], func=ACT.Abs, bias=bias[:, t:t + 1], scale=63.0
                )
            atiles[j] = a

        def hat(g):
            e = epool.tile([P, B, 4], BF16, name="e%d" % g, tag="e", align_bytes=64)
            nc.vector.tensor_scalar(
                out=e[:].rearrange("p (c i) t -> p c t i", i=4),
                in0=atiles[g // 2][:, :, g % 2, :].rearrange("p t (c i) -> p c t i", i=4),
                scalar1=mx32,
                scalar2=negmn,
                op0=ALU.subtract,
                op1=ALU.min,
            )
            etiles[g] = e

        def quant(g):
            nc.vector.quantize_mx(
                out=codes[g][:].bitcast(FP8X4),
                scales=eplane[g][:],
                in_=etiles[g][:].rearrange("p n t -> p (n t)"),
            )

        def mx(g):
            for h in range(2):
                for nh in range(2):
                    cols = slice(h * P, (h + 1) * P)
                    nc.tensor.matmul_mx(
                        out=acc[h][nh][:],
                        lhsT=codes[g][:, cols].bitcast(FP8X4),
                        lhsT_scale=eplane[g][:, cols],
                        rhs=words[g // 2][:, g % 2, nh * N_CLS:(nh + 1) * N_CLS].bitcast(FP4X4),
                        rhs_scale=planes[(g // SUPER) % 2][:, g % SUPER, nh * 512:(nh + 1) * 512],
                        start=(g == 0),
                        stop=(g == GROUPS - 1),
                    )

        for m in range(4):
            rep(m)
        rep_after = dict((rep_sets[m - 4][-1] // 2, m) for m in range(5, len(rep_sets)))
        for j in range(PAIRS):
            g0 = 2 * j
            g1 = g0 + 1
            dist(j)
            if j == 0:
                rep(4)
                hat(g0)
                quant(g0)
                hat(g1)
                quant(g1)
            else:
                hat(g0)
                hat(g1)
                quant(g0)
                quant(g1)
            mx(g0)
            mx(g1)
            if g1 == SUPER - 1:
                load_scales(2 * SUPER, 3 * SUPER, 2)
                for jj in range(12, 16):
                    load_words(jj)
            if g1 == 2 * SUPER - 1:
                load_scales(3 * SUPER, 4 * SUPER, 2)
            if j in rep_after:
                rep(rep_after[j])

        for h in range(2):
            for nh in range(2):
                o = opool.tile([P, 512], F32, name="o%d%d" % (h, nh))
                if nh == 0:
                    nc.scalar.mul(out=o[:], in_=acc[h][nh][:], mul=-1.0)
                else:
                    nc.vector.tensor_scalar(out=o[:], in0=acc[h][nh][:], scalar1=-1.0, scalar2=None, op0=ALU.mult)
                nc.sync.dma_start(out=out[h * P:(h + 1) * P, nh * 512:(nh + 1) * 512], in_=o[:])
